import numpy as np
import ml_dtypes


def mxq(x, axis, fmt="e4m3"):
    dtype, down = {"e4m3": (ml_dtypes.float8_e4m3fn, 7), "e5m2": (ml_dtypes.float8_e5m2, 14)}[fmt]
    v = np.moveaxis(np.asarray(x, np.float32).astype(ml_dtypes.bfloat16).astype(np.float64), axis, -1)
    blocks = v.reshape(v.shape[:-1] + (-1, 32))
    amax = np.abs(blocks).max(-1, keepdims=True)
    byte = np.maximum(np.where(amax > 0, np.frexp(amax)[1] - 1 + 127, 0) - down, 1)
    scale = np.exp2(byte - 127.0)
    codes = (blocks / scale).astype(np.float32).astype(dtype).astype(np.float64)
    return np.moveaxis((codes * scale).reshape(v.shape), -1, axis)


WIDE = False


def mx_kscale(k):
    if not WIDE:
        return np.ones(k)
    levels = np.array([10, -10, 5, -5, 0])
    if k % 512:
        return np.exp2(np.random.permutation(np.resize(levels, k // 32))).repeat(32)
    a = np.empty((k // 512, 16))
    for p in range(k // 512):
        a[p, :8] = np.random.permutation(np.resize(levels, 8))
        for g in range(8):
            far = levels[np.abs(levels - a[p, g]) >= 10]
            a[p, g + 8] = far[np.random.randint(len(far))]
    return np.exp2(a.ravel()).repeat(32)


BF16 = ml_dtypes.bfloat16


def bf(x):
    return np.asarray(x, np.float32).astype(BF16)


def f64(x):
    return np.asarray(x).astype(np.float64)


L, B, E, H, D, C = 1024, 2, 1024, 8, 128, 512
F = H * D


def rope(z):
    theta = 10000.0 ** (-2.0 / D * np.arange(D // 2))
    ang = np.arange(L)[:, None] * theta[None, :]
    cos, sin = np.cos(ang), np.sin(ang)
    z2 = z.reshape(B, H, L, D // 2, 2)
    r0 = z2[..., 0] * cos - z2[..., 1] * sin
    r1 = z2[..., 0] * sin + z2[..., 1] * cos
    return np.stack([r0, r1], axis=-1).reshape(B, H, L, D)


def draw0():
    s = mx_kscale(E)
    return {"x": bf(np.random.standard_normal((L, B, E)) * s),
            "w": bf(np.random.standard_normal((F, E)) / np.sqrt(E) / s[None, :]),
            "bias": bf(np.random.standard_normal(F) * 0.2)}


def core(x, w, bias):
    y = (mxq(f64(x), 2, "e4m3") @ mxq(f64(w), 1, "e4m3").T) + f64(bias)
    z = y.reshape(L, B, H, D).transpose(1, 2, 0, 3)
    return rope(np.maximum(z, 0.0))


def e4m3fn_bytes(y):
    return np.clip(np.asarray(y, np.float64), -448.0, 448.0).astype(np.float32).astype(ml_dtypes.float8_e4m3fn).view(np.uint8)


def e4m3fn_values(b):
    return np.asarray(b, np.uint8).view(ml_dtypes.float8_e4m3fn).astype(np.float64)


def setup_inputs():
    d = draw0()
    x0 = np.asarray(d['x']).astype(np.float64)
    s = (np.max(np.abs(x0), axis=(0, 1), keepdims=True) / 448.0).astype(np.float32)
    out = {}
    for k, v in d.items():
        if k == 'x':
            out['x_bytes'] = e4m3fn_bytes(x0 / s.astype(np.float64))
            out['x_scale'] = s
        else:
            out[k] = v
    return out


def reference(x_bytes, x_scale, w, bias):
    return core(e4m3fn_values(x_bytes) * x_scale.astype(np.float64), w, bias)

@@ -1,0 +1,278 @@
+from contextlib import ExitStack
+import math
+
+import concourse.mybir as mybir
+from concourse.masks import make_identity
+
+L, B, E, H, D = 1024, 2, 1024, 8, 128
+FLOPS = 2 * L * B * E * H * D
+
+F32 = mybir.dt.float32
+BF16 = mybir.dt.bfloat16
+U8 = mybir.dt.uint8
+U32 = mybir.dt.uint32
+I32 = mybir.dt.int32
+FP8 = mybir.dt.float8_e4m3fn
+FP8X4 = mybir.dt.float8_e4m3fn_x4
+ALU = mybir.AluOpType
+ACT = mybir.ActivationFunctionType
+
+P = 128
+PASSES = E // 512
+TWO_PI = 2.0 * math.pi
+
+
+def tile_weightlinearattention_pa_kernel(tc, x_bytes, x_scale, w, bias, out):
+    nc = tc.nc
+    with ExitStack() as ctx:
+        const = ctx.enter_context(tc.tile_pool(name="const", bufs=1))
+        raw = ctx.enter_context(tc.tile_pool(name="raw", bufs=1))
+        work = ctx.enter_context(tc.tile_pool(name="work", bufs=2))
+        psum = ctx.enter_context(tc.psum_pool(name="psum", bufs=2))
+
+        sc_col = const.tile([P, E // P], F32, name="sc_col")
+        bias_bf = const.tile([P, H], BF16, name="bias_bf")
+        with nc.allow_non_contiguous_dma(reason="one value to a partition"):
+            nc.scalar.dma_start(out=sc_col[:], in_=x_scale.rearrange("a b (k p) -> p (a b k)", p=P))
+            nc.scalar.dma_start(out=bias_bf[:], in_=bias.rearrange("(h d) -> d h", d=D))
+
+        xb = [None] * 8
+        wr = [None] * 8
+
+        def load_x(q):
+            xb[q] = raw.tile([P, B, E], U8, name="xbytes%d" % q)
+            nc.sync.dma_start(out=xb[q][:], in_=x_bytes[q * P:(q + 1) * P, :, :])
+
+        def load_w(h):
+            wr[h] = raw.tile([P, E], BF16, name="wraw%d" % h)
+            nc.sync.dma_start(out=wr[h][:], in_=w[h * P:(h + 1) * P, :])
+
+        load_x(0)
+        load_x(1)
+        for h in range(8):
+            load_w(h)
+        for q in range(2, 8):
+            load_x(q)
+
+        zero = const.tile([P, 1], F32, name="zero")
+        nc.gpsimd.memset(zero[:], 0.0)
+        ident = const.tile([P, P], F32, name="ident")
+        make_identity(nc, ident[:])
+        swap = const.tile([P, P], F32, name="swap")
+        iv = ident[:].rearrange("p (i e) -> p i e", e=2)
+        sv = swap[:].rearrange("p (i e) -> p i e", e=2)
+        pos = const.tile([P, L], F32, name="pos")
+        for a in range(2):
+            nc.gpsimd.iota(pos[:, 512 * a:512 * (a + 1)], pattern=[[1, 512]], base=512 * a, channel_multiplier=0,
+                           allow_small_or_imprecise_dtypes=True)
+
+        scale_all = const.tile([P, E], F32, name="scale_all")
+        warm = const.tile([P, 1], F32, name="warm")
+        trow = const.tile([P, D], F32, name="trow")
+        tdiag = const.tile([P, D], F32, name="tdiag")
+        theta = const.tile([P, 1], F32, name="theta")
+        turns = const.tile([P, 1], F32, name="turns")
+        kint = const.tile([P, L], I32, name="kint")
+        ang = const.tile([P, L], F32, name="ang")
+        aabs = const.tile([P, L], F32, name="aabs")
+        tab = const.tile([P, 2, L], F32, name="tab")
+        bias_f = const.tile([P, H], F32, name="bias_f")
+
+        def spread_scales():
+            for b in range(2):
+                tp = psum.tile([P, 4, P], F32, name="tp", tag="tp", bufs=2)
+                for i in range(4):
+                    k = 4 * b + i
+                    nc.tensor.transpose(tp[:, i, :], sc_col[:, k:k + 1].to_broadcast([P, P]), ident[:])
+                nc.scalar.copy(out=scale_all[:, 512 * b:512 * (b + 1)], in_=tp[:].rearrange("p i j -> p (i j)"))
+
+        def tables_vector():
+            nc.vector.memset(trow[:, 0:1], 1.0)
+            nc.vector.memset(trow[:, 1:2], -1.0)
+            m = 2
+            while m < D:
+                nc.vector.tensor_scalar(out=trow[:, m:2 * m], in0=trow[:, 0:m],
+                                        scalar1=10000.0 ** (-(m // 2) / 64.0), scalar2=None, op0=ALU.mult)
+                m = 2 * m
+            nc.vector.tensor_tensor(out=tdiag[:], in0=trow[:], in1=ident[:], op=ALU.mult)
+            nc.vector.reduce_sum(out=theta[:], in_=tdiag[:], axis=mybir.AxisListType.X)
+            nc.vector.tensor_scalar(out=turns[:], in0=theta[:], scalar1=1.0 / TWO_PI, scalar2=None, op0=ALU.mult)
+            for a in range(2):
+                cols = slice(512 * a, 512 * (a + 1))
+                nc.vector.tensor_scalar(out=kint[:, cols], in0=pos[:, cols], scalar1=turns[:, 0:1], scalar2=None,
+                                        op0=ALU.mult)
+                nc.vector.scalar_tensor_tensor(out=ang[:, cols], in0=pos[:, cols], scalar=turns[:, 0:1],
+                                               in1=kint[:, cols], op0=ALU.mult, op1=ALU.subtract)
+            nc.vector.tensor_copy(out=sv[:, :, 0:1], in_=iv[:, :, 1:2])
+            nc.vector.tensor_copy(out=sv[:, :, 1:2], in_=iv[:, :, 0:1])
+            nc.vector.tensor_copy(out=bias_f[:], in_=bias_bf[:])
+
+        def tables_scalar(a):
+            cols = slice(256 * a, 256 * (a + 1))
+            nc.scalar.activation(out=aabs[:, cols], in_=ang[:, cols], func=ACT.Abs)
+            nc.scalar.activation(out=tab[:, 1, cols], in_=ang[:, cols], func=ACT.Sin, scale=TWO_PI)
+            nc.scalar.activation(out=tab[:, 0, cols], in_=aabs[:, cols], func=ACT.Sin, bias=math.pi / 2.0,
+                                 scale=-TWO_PI)
+
+        wc = [const.tile([P, 4, PASSES * P], U32, name="wc%d" % a, align_bytes=64) for a in range(2)]
+        ws = [const.tile([P, 4, PASSES * P], U8, name="ws%d" % a, align_bytes=64) for a in range(2)]
+        xc = [const.tile([P, PASSES, 256], U32, name="xc%d" % j, align_bytes=64) for j in range(8)]
+        xs = [const.tile([P, PASSES, 256], U8, name="xs%d" % j, align_bytes=64) for j in range(8)]
+        wg = [None] * 8
+        xw = [None] * 16
+        xg = [None] * 8
+        rs = [None] * 32
+        uv = [None] * 32
+        later = []
+
+        def turn(src):
+            words = src.bitcast(F32)
+            tp = psum.tile([P, PASSES, 2, P], F32, name="tp", tag="tp", bufs=2)
+            for g in range(PASSES):
+                for u in range(2):
+                    nc.tensor.transpose(tp[:, g, u, :], words[:, 256 * g + u:256 * (g + 1):2], ident[:])
+            return tp
+
+        def w_turn(h):
+            tp = turn(wr[h][:])
+            if h % 4 == 0:
+                wg[h // 4] = work.tile([P, 4, PASSES, P, 4], BF16, name="wg", tag="wg", bufs=2, align_bytes=64)
+            nc.scalar.copy(out=wg[h // 4][:, h % 4].bitcast(F32), in_=tp[:].rearrange("p g u r -> p g r u"))
+
+        def w_quant(a):
+            nc.vector.quantize_mx(out=wc[a][:].rearrange("p a n -> p (a n)").bitcast(FP8X4),
+                                  scales=ws[a][:].rearrange("p a n -> p (a n)"),
+                                  in_=wg[a][:].rearrange("p a g r j -> p (a g r j)"))
+
+        def x_widen(j):
+            c = j % 2
+            for i in range(2):
+                q = 2 * (j // 2) + i
+                xw[2 * j + i] = work.tile([P, E], BF16, name="xw", tag="xw", bufs=4)
+                nc.vector.tensor_tensor(out=xw[2 * j + i][:], in0=xb[q][:, c, :].bitcast(FP8),
+                                        in1=scale_all[:], op=ALU.mult)
+
+        def x_turn(j):
+            xg[j] = work.tile([P, PASSES, 2, P, 4], BF16, name="xg", tag="xg", bufs=3, align_bytes=64)
+            for i in range(2):
+                tp = turn(xw[2 * j + i][:])
+                nc.scalar.copy(out=xg[j][:, :, i, :, :].bitcast(F32), in_=tp[:].rearrange("p g u r -> p g r u"))
+
+        def x_quant(j):
+            nc.vector.quantize_mx(out=xc[j][:].rearrange("p g n -> p (g n)").bitcast(FP8X4),
+                                  scales=xs[j][:].rearrange("p g n -> p (g n)"),
+                                  in_=xg[j][:].rearrange("p g t r j -> p (g t r j)"))
+
+        def mx_relu(j, halves=(0, 1)):
+            for hp in [2 * a + b for a in halves for b in range(2)]:
+                y = psum.tile([P, 2, 256], F32, name="y", tag="y", bufs=3)
+                for hh in range(2):
+                    h = 2 * hp + hh
+                    for g in range(PASSES):
+                        nc.tensor.matmul_mx(out=y[:, hh, :],
+                                            lhsT=wc[h // 4][:, h % 4, g * P:(g + 1) * P].bitcast(FP8X4),
+                                            lhsT_scale=ws[h // 4][:, h % 4, g * P:(g + 1) * P],
+                                            rhs=xc[j][:, g, :].bitcast(FP8X4),
+                                            rhs_scale=xs[j][:, g, :],
+                                            start=(g == 0), stop=(g == PASSES - 1))
+                if hp % 2 == 0:
+                    rs[2 * j + hp // 2] = work.tile([P, 4, 256], F32, name="r", tag="r", bufs=6)
+                for hh in range(2):
+                    h = 2 * hp + hh
+                    nc.scalar.activation(out=rs[2 * j + hp // 2][:, h % 4, :], in_=y[:, hh, :], func=ACT.Relu,
+                                         bias=bias_f[:, h:h + 1], scale=1.0)
+
+        def product(j, quad):
+            n0 = 256 * (j // 2)
+            uv[2 * j + quad] = work.tile([P, 2, 4, 256], F32, name="uv", tag="uv", bufs=4)
+            nc.vector.tensor_tensor(out=uv[2 * j + quad][:],
+                                    in0=rs[2 * j + quad][:].unsqueeze(1).to_broadcast([P, 2, 4, 256]),
+                                    in1=tab[:, :, n0:n0 + 256].unsqueeze(2).to_broadcast([P, 2, 4, 256]),
+                                    op=ALU.mult)
+
+        def last_heads(j, quad):
+            c = j % 2
+            n0 = 256 * (j // 2)
+            tags = [("y", 3), ("y", 3), ("y", 3), ("tp", 2), ("tp", 2), ("ot", 3), ("y", 3), ("y", 3)]
+            for a in range(4):
+                src = rs[2 * j + quad]
+                one = work.tile([P, 2, 256], F32, name="one", tag="one", bufs=4)
+                nc.vector.tensor_tensor(out=one[:], in0=src[:, a, :].unsqueeze(1).to_broadcast([P, 2, 256]),
+                                        in1=tab[:, :, n0:n0 + 256], op=ALU.mult)
+                for t in range(2):
+                    tag, nbufs = tags[2 * a + t]
+                    ot = psum.tile([P, P], F32, name=tag, tag=tag, bufs=nbufs)
+                    nc.tensor.matmul(out=ot[:], lhsT=one[:, 0, t * P:(t + 1) * P], rhs=ident[:],
+                                     is_transpose=True, start=True, stop=False)
+                    nc.tensor.matmul(out=ot[:], lhsT=one[:, 1, t * P:(t + 1) * P], rhs=swap[:],
+                                     is_transpose=True, start=False, stop=True)
+                    o = work.tile([P, P], F32, name="os", tag="os", bufs=8)
+                    nc.scalar.copy(out=o[:], in_=ot[:])
+                    nt = n0 + t * P
+                    nc.sync.dma_start(out=out[c, 4 * quad + a, nt:nt + P, :], in_=o[:])
+
+        def turn_out(j, quad, on_vector):
+            c = j % 2
+            for t in range(2):
+                ot = psum.tile([P, 4, P], F32, name="ot", tag="ot", bufs=3)
+                for k in range(4):
+                    src = uv[2 * j + quad]
+                    nc.tensor.matmul(out=ot[:, k, :], lhsT=src[:, 0, k, t * P:(t + 1) * P], rhs=ident[:],
+                                     is_transpose=True, start=True, stop=False)
+                    nc.tensor.matmul(out=ot[:, k, :], lhsT=src[:, 1, k, t * P:(t + 1) * P], rhs=swap[:],
+                                     is_transpose=True, start=False, stop=True)
+                nt = 256 * (j // 2) + t * P
+                dst = out[c, 4 * quad:4 * quad + 4, nt:nt + P, :].rearrange("h n d -> n h d")
+                if on_vector:
+                    later.append((ot, dst))
+                else:
+                    o = work.tile([P, 4, P], F32, name="o", tag="o", bufs=8)
+                    nc.scalar.copy(out=o[:], in_=ot[:])
+                    nc.sync.dma_start(out=dst, in_=o[:])
+
+        def finish_on_vector():
+            for ot, dst in later:
+                o = work.tile([P, 4, P], F32, name="o", tag="o", bufs=8)
+                nc.vector.tensor_copy(out=o[:], in_=ot[:])
+                nc.sync.dma_start(out=dst, in_=o[:])
+            later.clear()
+
+        with tc.manual_schedule():
+            nc.scalar.activation(out=warm[:], in_=zero[:], func=ACT.Sin)
+            spread_scales()
+            tables_vector()
+            for h in range(4):
+                w_turn(h)
+            tables_scalar(0)
+            x_widen(0)
+            x_turn(0)
+            x_widen(1)
+            x_turn(1)
+            w_quant(0)
+            x_quant(0)
+            for h in range(4, 8):
+                w_turn(h)
+            mx_relu(0, (0,))
+            x_widen(2)
+            x_turn(2)
+            w_quant(1)
+            mx_relu(0, (1,))
+            for k in range(8):
+                if k < 3:
+                    tables_scalar(k + 1)
+                if 1 <= k < 6:
+                    x_widen(k + 2)
+                    x_turn(k + 2)
+                if k < 7:
+                    x_quant(k + 1)
+                    mx_relu(k + 1)
+                if k >= 1:
+                    turn_out(k - 1, 0, False)
+                    turn_out(k - 1, 1, False)
+                product(k, 0)
+                if k < 7:
+                    product(k, 1)
+                else:
+                    turn_out(k, 0, True)
+                    last_heads(k, 1)
+                    finish_on_vector()

@@ -75,12 +75,24 @@ def tile_weightlinearattention_pa_kernel(tc, x_bytes, x_scale, w, bias, out):
         kint = const.tile([P, L], I32, name="kint")
         ang = const.tile([P, L], F32, name="ang")
         aabs = const.tile([P, L], F32, name="aabs")
-        tab = const.tile([P, 2, L], F32, name="tab")
+        tab = const.tile([P, 4, 2, 256], F32, name="tab")
+        junk = const.tile([P, 16], U32, name="junk")
         bias_f = const.tile([P, H], F32, name="bias_f")
+
+        depth = {"tabp": 1, "tp": 1, "y": 3, "ot": 3}
+        head_cycle = ["tp", "ot", "y", "ot", "y", "ot", "y"]
+        head_used = []
+
+        def head_tag():
+            head_used.append(0)
+            return head_cycle[(len(head_used) - 1) % len(head_cycle)]
+
+        def bank(shape, tag):
+            return psum.tile(shape, F32, name=tag, tag=tag, bufs=depth[tag])
 
         def spread_scales():
             for b in range(2):
-                tp = psum.tile([P, 4, P], F32, name="tp", tag="tp", bufs=2)
+                tp = bank([P, 4, P], head_tag())
                 for i in range(4):
                     k = 4 * b + i
                     nc.tensor.transpose(tp[:, i, :], sc_col[:, k:k + 1].to_broadcast([P, P]), ident[:])
@@ -110,8 +122,8 @@ def tile_weightlinearattention_pa_kernel(tc, x_bytes, x_scale, w, bias, out):
         def tables_scalar(a):
             cols = slice(256 * a, 256 * (a + 1))
             nc.scalar.activation(out=aabs[:, cols], in_=ang[:, cols], func=ACT.Abs)
-            nc.scalar.activation(out=tab[:, 1, cols], in_=ang[:, cols], func=ACT.Sin, scale=TWO_PI)
-            nc.scalar.activation(out=tab[:, 0, cols], in_=aabs[:, cols], func=ACT.Sin, bias=math.pi / 2.0,
+            nc.scalar.activation(out=tab[:, a, 1, :], in_=ang[:, cols], func=ACT.Sin, scale=TWO_PI)
+            nc.scalar.activation(out=tab[:, a, 0, :], in_=aabs[:, cols], func=ACT.Sin, bias=math.pi / 2.0,
                                  scale=-TWO_PI)
 
         wc = [const.tile([P, 4, PASSES * P], U32, name="wc%d" % a, align_bytes=64) for a in range(2)]
@@ -122,19 +134,22 @@ def tile_weightlinearattention_pa_kernel(tc, x_bytes, x_scale, w, bias, out):
         xw = [None] * 16
         xg = [None] * 8
         rs = [None] * 32
-        uv = [None] * 32
+        uva = [None] * 8
+        uvb = [None] * 8
+        uvg = [None] * 8
+        tabp = [None] * 4
         later = []
 
-        def turn(src):
+        def turn(src, tag):
             words = src.bitcast(F32)
-            tp = psum.tile([P, PASSES, 2, P], F32, name="tp", tag="tp", bufs=2)
+            tp = bank([P, PASSES, 2, P], tag)
             for g in range(PASSES):
                 for u in range(2):
                     nc.tensor.transpose(tp[:, g, u, :], words[:, 256 * g + u:256 * (g + 1):2], ident[:])
             return tp
 
         def w_turn(h):
-            tp = turn(wr[h][:])
+            tp = turn(wr[h][:], head_tag())
             if h % 4 == 0:
                 wg[h // 4] = work.tile([P, 4, PASSES, P, 4], BF16, name="wg", tag="wg", bufs=2, align_bytes=64)
             nc.scalar.copy(out=wg[h // 4][:, h % 4].bitcast(F32), in_=tp[:].rearrange("p g u r -> p g r u"))
@@ -152,11 +167,11 @@ def tile_weightlinearattention_pa_kernel(tc, x_bytes, x_scale, w, bias, out):
                 nc.vector.tensor_tensor(out=xw[2 * j + i][:], in0=xb[q][:, c, :].bitcast(FP8),
                                         in1=scale_all[:], op=ALU.mult)
 
-        def x_turn(j):
-            xg[j] = work.tile([P, PASSES, 2, P, 4], BF16, name="xg", tag="xg", bufs=3, align_bytes=64)
-            for i in range(2):
-                tp = turn(xw[2 * j + i][:])
-                nc.scalar.copy(out=xg[j][:, :, i, :, :].bitcast(F32), in_=tp[:].rearrange("p g u r -> p g r u"))
+        def x_turn(j, i, tag):
+            if i == 0:
+                xg[j] = work.tile([P, PASSES, 2, P, 4], BF16, name="xg", tag="xg", bufs=3, align_bytes=64)
+            tp = turn(xw[2 * j + i][:], tag)
+            nc.scalar.copy(out=xg[j][:, :, i, :, :].bitcast(F32), in_=tp[:].rearrange("p g u r -> p g r u"))
 
         def x_quant(j):
             nc.vector.quantize_mx(out=xc[j][:].rearrange("p g n -> p (g n)").bitcast(FP8X4),
@@ -165,7 +180,7 @@ def tile_weightlinearattention_pa_kernel(tc, x_bytes, x_scale, w, bias, out):
 
         def mx_relu(j, halves=(0, 1)):
             for hp in [2 * a + b for a in halves for b in range(2)]:
-                y = psum.tile([P, 2, 256], F32, name="y", tag="y", bufs=3)
+                y = bank([P, 2, 256], "y")
                 for hh in range(2):
                     h = 2 * hp + hh
                     for g in range(PASSES):
@@ -182,45 +197,61 @@ def tile_weightlinearattention_pa_kernel(tc, x_bytes, x_scale, w, bias, out):
                     nc.scalar.activation(out=rs[2 * j + hp // 2][:, h % 4, :], in_=y[:, hh, :], func=ACT.Relu,
                                          bias=bias_f[:, h:h + 1], scale=1.0)
 
-        def product(j, quad):
-            n0 = 256 * (j // 2)
-            uv[2 * j + quad] = work.tile([P, 2, 4, 256], F32, name="uv", tag="uv", bufs=4)
-            nc.vector.tensor_tensor(out=uv[2 * j + quad][:],
-                                    in0=rs[2 * j + quad][:].unsqueeze(1).to_broadcast([P, 2, 4, 256]),
-                                    in1=tab[:, :, n0:n0 + 256].unsqueeze(2).to_broadcast([P, 2, 4, 256]),
-                                    op=ALU.mult)
+        def fill_tables(blk):
+            tabp[blk] = bank([P, 2, 256], "tabp")
+            nc.tensor.matmul(out=tabp[blk][:].rearrange("p e n -> p (e n)"), lhsT=ident[:],
+                             rhs=tab[:, blk].rearrange("p e n -> p (e n)"), start=True, stop=True)
 
-        def last_heads(j, quad):
+        def vec_product(dst, r, heads, blk):
+            nc.vector.tensor_tensor(out=dst, in0=r.unsqueeze(1).to_broadcast([P, 2, heads, 256]),
+                                    in1=tabp[blk][:].unsqueeze(2).to_broadcast([P, 2, heads, 256]), op=ALU.mult)
+
+        def pool_product(dst, r, heads, blk):
+            nc.gpsimd.tensor_tensor(out=dst, in0=r.unsqueeze(1).to_broadcast([P, 2, heads, 256]),
+                                    in1=tab[:, blk].unsqueeze(2).to_broadcast([P, 2, heads, 256]), op=ALU.mult)
+
+        def pool_gate(j):
+            nc.gpsimd.tensor_copy(out=junk[:], in_=xc[j][:, 0, 0:16])
+
+        def product(j):
+            blk = j // 2
+            uva[j] = work.tile([P, 2, 4, 256], F32, name="uva", tag="uva", bufs=3)
+            uvb[j] = work.tile([P, 2, 2, 256], F32, name="uvb", tag="uvb", bufs=3)
+            uvg[j] = work.tile([P, 2, 2, 256], F32, name="uvg", tag="uvg", bufs=3)
+            pool_product(uvg[j][:], rs[2 * j + 1][:, 2:4, :], 2, blk)
+            vec_product(uva[j][:], rs[2 * j][:], 4, blk)
+            vec_product(uvb[j][:], rs[2 * j + 1][:, 0:2, :], 2, blk)
+
+        def head_src(j, h):
+            if h < 4:
+                return uva[j][:, :, h, :]
+            if h < 6:
+                return uvb[j][:, :, h - 4, :]
+            return uvg[j][:, :, h - 6, :]
+
+        def add_turned(dst, both, t):
+            nc.tensor.matmul(out=dst, lhsT=both[:, 0, t * P:(t + 1) * P], rhs=ident[:],
+                             is_transpose=True, start=True, stop=False)
+            nc.tensor.matmul(out=dst, lhsT=both[:, 1, t * P:(t + 1) * P], rhs=swap[:],
+                             is_transpose=True, start=False, stop=True)
+
+        def last_head(j, h, both, tags):
             c = j % 2
             n0 = 256 * (j // 2)
-            tags = [("y", 3), ("y", 3), ("y", 3), ("tp", 2), ("tp", 2), ("ot", 3), ("y", 3), ("y", 3)]
-            for a in range(4):
-                src = rs[2 * j + quad]
-                one = work.tile([P, 2, 256], F32, name="one", tag="one", bufs=4)
-                nc.vector.tensor_tensor(out=one[:], in0=src[:, a, :].unsqueeze(1).to_broadcast([P, 2, 256]),
-                                        in1=tab[:, :, n0:n0 + 256], op=ALU.mult)
-                for t in range(2):
-                    tag, nbufs = tags[2 * a + t]
-                    ot = psum.tile([P, P], F32, name=tag, tag=tag, bufs=nbufs)
-                    nc.tensor.matmul(out=ot[:], lhsT=one[:, 0, t * P:(t + 1) * P], rhs=ident[:],
-                                     is_transpose=True, start=True, stop=False)
-                    nc.tensor.matmul(out=ot[:], lhsT=one[:, 1, t * P:(t + 1) * P], rhs=swap[:],
-                                     is_transpose=True, start=False, stop=True)
-                    o = work.tile([P, P], F32, name="os", tag="os", bufs=8)
-                    nc.scalar.copy(out=o[:], in_=ot[:])
-                    nt = n0 + t * P
-                    nc.sync.dma_start(out=out[c, 4 * quad + a, nt:nt + P, :], in_=o[:])
+            for t in range(2):
+                ot = bank([P, P], tags[t])
+                add_turned(ot[:], both, t)
+                o = work.tile([P, P], F32, name="os", tag="os", bufs=8)
+                nc.scalar.copy(out=o[:], in_=ot[:])
+                nt = n0 + t * P
+                nc.sync.dma_start(out=out[c, h, nt:nt + P, :], in_=o[:])
 
         def turn_out(j, quad, on_vector):
             c = j % 2
             for t in range(2):
-                ot = psum.tile([P, 4, P], F32, name="ot", tag="ot", bufs=3)
+                ot = bank([P, 4, P], "ot")
                 for k in range(4):
-                    src = uv[2 * j + quad]
-                    nc.tensor.matmul(out=ot[:, k, :], lhsT=src[:, 0, k, t * P:(t + 1) * P], rhs=ident[:],
-                                     is_transpose=True, start=True, stop=False)
-                    nc.tensor.matmul(out=ot[:, k, :], lhsT=src[:, 1, k, t * P:(t + 1) * P], rhs=swap[:],
-                                     is_transpose=True, start=False, stop=True)
+                    add_turned(ot[:, k, :], head_src(j, 4 * quad + k), t)
                 nt = 256 * (j // 2) + t * P
                 dst = out[c, 4 * quad:4 * quad + 4, nt:nt + P, :].rearrange("h n d -> n h d")
                 if on_vector:
@@ -244,35 +275,50 @@ def tile_weightlinearattention_pa_kernel(tc, x_bytes, x_scale, w, bias, out):
             for h in range(4):
                 w_turn(h)
             tables_scalar(0)
-            x_widen(0)
-            x_turn(0)
-            x_widen(1)
-            x_turn(1)
+            for j in range(2):
+                x_widen(j)
+                for i in range(2):
+                    x_turn(j, i, head_tag())
+            fill_tables(0)
             w_quant(0)
             x_quant(0)
             for h in range(4, 8):
                 w_turn(h)
             mx_relu(0, (0,))
             x_widen(2)
-            x_turn(2)
+            for i in range(2):
+                x_turn(2, i, ("tp", "ot")[i])
             w_quant(1)
             mx_relu(0, (1,))
-            for k in range(8):
+            for k in range(7):
                 if k < 3:
                     tables_scalar(k + 1)
                 if 1 <= k < 6:
                     x_widen(k + 2)
-                    x_turn(k + 2)
-                if k < 7:
-                    x_quant(k + 1)
-                    mx_relu(k + 1)
+                    x_turn(k + 2, 0, "tp")
+                x_quant(k + 1)
+                pool_gate(k + 1)
+                mx_relu(k + 1)
+                if 1 <= k < 6:
+                    x_turn(k + 2, 1, "tp")
                 if k >= 1:
                     turn_out(k - 1, 0, False)
+                product(k)
+                if k % 2 == 1:
+                    fill_tables((k + 1) // 2)
+                if k >= 1:
                     turn_out(k - 1, 1, False)
-                product(k, 0)
-                if k < 7:
-                    product(k, 1)
-                else:
-                    turn_out(k, 0, True)
-                    last_heads(k, 1)
-                    finish_on_vector()
+            ones = [work.tile([P, 2, 256], F32, name="one", tag="one", bufs=4) for h in range(4, 8)]
+            for h in (6, 7):
+                pool_product(ones[h - 4][:].unsqueeze(2), rs[15][:, h - 4:h - 3, :], 1, 3)
+            turn_out(6, 0, False)
+            uva[7] = work.tile([P, 2, 4, 256], F32, name="uva", tag="uva", bufs=3)
+            vec_product(uva[7][:], rs[14][:], 4, 3)
+            turn_out(6, 1, False)
+            last_head(7, 6, ones[2], ("y", "y"))
+            last_head(7, 7, ones[3], ("y", "tp"))
+            turn_out(7, 0, True)
+            for h in (4, 5):
+                vec_product(ones[h - 4][:].unsqueeze(2), rs[15][:, h - 4:h - 3, :], 1, 3)
+                last_head(7, h, ones[h - 4], (("y", "y"), ("y", "tp"))[h - 4])
+            finish_on_vector()

@@ -77,6 +77,7 @@ def tile_weightlinearattention_pa_kernel(tc, x_bytes, x_scale, w, bias, out):
         aabs = const.tile([P, L], F32, name="aabs")
         tab = const.tile([P, 4, 2, 256], F32, name="tab")
         junk = const.tile([P, 16], U32, name="junk")
+        junk_bf = const.tile([P, 16], BF16, name="junk_bf")
         bias_f = const.tile([P, H], F32, name="bias_f")
 
         depth = {"tabp": 1, "tp": 1, "y": 3, "ot": 3}
@@ -178,8 +179,8 @@ def tile_weightlinearattention_pa_kernel(tc, x_bytes, x_scale, w, bias, out):
                                   scales=xs[j][:].rearrange("p g n -> p (g n)"),
                                   in_=xg[j][:].rearrange("p g t r j -> p (g t r j)"))
 
-        def mx_relu(j, halves=(0, 1)):
-            for hp in [2 * a + b for a in halves for b in range(2)]:
+        def mx_relu(j, pairs):
+            for hp in pairs:
                 y = bank([P, 2, 256], "y")
                 for hh in range(2):
                     h = 2 * hp + hh
@@ -210,8 +211,11 @@ def tile_weightlinearattention_pa_kernel(tc, x_bytes, x_scale, w, bias, out):
             nc.gpsimd.tensor_tensor(out=dst, in0=r.unsqueeze(1).to_broadcast([P, 2, heads, 256]),
                                     in1=tab[:, blk].unsqueeze(2).to_broadcast([P, 2, heads, 256]), op=ALU.mult)
 
-        def pool_gate(j):
-            nc.gpsimd.tensor_copy(out=junk[:], in_=xc[j][:, 0, 0:16])
+        def pool_gate(k):
+            if 1 <= k < 6:
+                nc.gpsimd.tensor_copy(out=junk_bf[:], in_=xw[2 * (k + 2) + 1][:, 0:16])
+            else:
+                nc.gpsimd.tensor_copy(out=junk[:], in_=xc[k + 1][:, 0, 0:16])
 
         def product(j):
             blk = j // 2
@@ -246,9 +250,9 @@ def tile_weightlinearattention_pa_kernel(tc, x_bytes, x_scale, w, bias, out):
                 nt = n0 + t * P
                 nc.sync.dma_start(out=out[c, h, nt:nt + P, :], in_=o[:])
 
-        def turn_out(j, quad, on_vector):
+        def turn_out(j, quad, on_vector, tiles=(0, 1)):
             c = j % 2
-            for t in range(2):
+            for t in tiles:
                 ot = bank([P, 4, P], "ot")
                 for k in range(4):
                     add_turned(ot[:, k, :], head_src(j, 4 * quad + k), t)
@@ -284,30 +288,28 @@ def tile_weightlinearattention_pa_kernel(tc, x_bytes, x_scale, w, bias, out):
             x_quant(0)
             for h in range(4, 8):
                 w_turn(h)
-            mx_relu(0, (0,))
+            mx_relu(0, (0, 1))
             x_widen(2)
             for i in range(2):
                 x_turn(2, i, ("tp", "ot")[i])
             w_quant(1)
-            mx_relu(0, (1,))
+            mx_relu(0, (2, 3))
             for k in range(7):
                 if k < 3:
                     tables_scalar(k + 1)
+                x_quant(k + 1)
                 if 1 <= k < 6:
                     x_widen(k + 2)
-                    x_turn(k + 2, 0, "tp")
-                x_quant(k + 1)
-                pool_gate(k + 1)
-                mx_relu(k + 1)
-                if 1 <= k < 6:
-                    x_turn(k + 2, 1, "tp")
-                if k >= 1:
-                    turn_out(k - 1, 0, False)
+                pool_gate(k)
+                for i in range(4):
+                    if k >= 1:
+                        turn_out(k - 1, i // 2, False, (i % 2,))
+                    mx_relu(k + 1, (i,))
+                    if i == 0 and k in (2, 4, 6):
+                        fill_tables(k // 2)
+                    if i < 2 and 1 <= k < 6:
+                        x_turn(k + 2, i, "tp")
                 product(k)
-                if k % 2 == 1:
-                    fill_tables((k + 1) // 2)
-                if k >= 1:
-                    turn_out(k - 1, 1, False)
             ones = [work.tile([P, 2, 256], F32, name="one", tag="one", bufs=4) for h in range(4, 8)]
             for h in (6, 7):
                 pool_product(ones[h - 4][:].unsqueeze(2), rs[15][:, h - 4:h - 3, :], 1, 3)

@@ -76,6 +76,7 @@ def tile_weightlinearattention_pa_kernel(tc, x_bytes, x_scale, w, bias, out):
         ang = const.tile([P, L], F32, name="ang")
         aabs = const.tile([P, L], F32, name="aabs")
         tab = const.tile([P, 4, 2, 256], F32, name="tab")
+        idle = const.tile([P, 512], BF16, name="idle")
         junk = const.tile([P, 16], U32, name="junk")
         junk_bf = const.tile([P, 16], BF16, name="junk_bf")
         bias_f = const.tile([P, H], F32, name="bias_f")
@@ -90,6 +91,10 @@ def tile_weightlinearattention_pa_kernel(tc, x_bytes, x_scale, w, bias, out):
 
         def bank(shape, tag):
             return psum.tile(shape, F32, name=tag, tag=tag, bufs=depth[tag])
+
+        def keep_clock(n):
+            for i in range(n):
+                nc.tensor.matmul(out=spare[0][:], lhsT=idle[:, 0:P], rhs=idle[:], start=True, stop=True)
 
         def spread_scales():
             for b in range(2):
@@ -139,6 +144,7 @@ def tile_weightlinearattention_pa_kernel(tc, x_bytes, x_scale, w, bias, out):
         uvb = [None] * 8
         uvg = [None] * 8
         tabp = [None] * 4
+        spare = []
         later = []
 
         def turn(src, tag):
@@ -274,20 +280,29 @@ def tile_weightlinearattention_pa_kernel(tc, x_bytes, x_scale, w, bias, out):
 
         with tc.manual_schedule():
             nc.scalar.activation(out=warm[:], in_=zero[:], func=ACT.Sin)
+            nc.vector.memset(idle[:], 0.0)
+            spare.append(bank([P, 512], "tabp"))
+            keep_clock(5)
             spread_scales()
+            keep_clock(1)
             tables_vector()
             for h in range(4):
                 w_turn(h)
+                if h % 2 == 1:
+                    keep_clock(1)
             tables_scalar(0)
             for j in range(2):
                 x_widen(j)
                 for i in range(2):
                     x_turn(j, i, head_tag())
-            fill_tables(0)
+                    keep_clock(1)
             w_quant(0)
             x_quant(0)
             for h in range(4, 8):
                 w_turn(h)
+                if h == 5:
+                    keep_clock(1)
+            fill_tables(0)
             mx_relu(0, (0, 1))
             x_widen(2)
             for i in range(2):

@@ -61,20 +61,18 @@ def tile_weightlinearattention_pa_kernel(tc, x_bytes, x_scale, w, bias, out):
         swap = const.tile([P, P], F32, name="swap")
         iv = ident[:].rearrange("p (i e) -> p i e", e=2)
         sv = swap[:].rearrange("p (i e) -> p i e", e=2)
-        pos = const.tile([P, L], F32, name="pos")
-        for a in range(2):
-            nc.gpsimd.iota(pos[:, 512 * a:512 * (a + 1)], pattern=[[1, 512]], base=512 * a, channel_multiplier=0,
-                           allow_small_or_imprecise_dtypes=True)
+        pos = const.tile([P, L // P], F32, name="pos")
+        nc.gpsimd.iota(pos[:], pattern=[[P, L // P]], base=0, channel_multiplier=1,
+                       allow_small_or_imprecise_dtypes=True)
 
         scale_all = const.tile([P, E], F32, name="scale_all")
         warm = const.tile([P, 1], F32, name="warm")
         trow = const.tile([P, D], F32, name="trow")
-        tdiag = const.tile([P, D], F32, name="tdiag")
-        theta = const.tile([P, 1], F32, name="theta")
-        turns = const.tile([P, 1], F32, name="turns")
-        kint = const.tile([P, L], I32, name="kint")
-        ang = const.tile([P, L], F32, name="ang")
-        aabs = const.tile([P, L], F32, name="aabs")
+        turns = const.tile([P, D], F32, name="turns")
+        kint = const.tile([P, L // P, D], I32, name="kint")
+        ang = const.tile([P, L // P, D], F32, name="ang")
+        aabs = const.tile([P, L // P, D], F32, name="aabs")
+        tab_t = const.tile([P, L // P, 2, D], F32, name="tab_t")
         tab = const.tile([P, 4, 2, 256], F32, name="tab")
         idle = const.tile([P, 512], BF16, name="idle")
         junk = const.tile([P, 16], U32, name="junk")
@@ -112,24 +110,22 @@ def tile_weightlinearattention_pa_kernel(tc, x_bytes, x_scale, w, bias, out):
                 nc.vector.tensor_scalar(out=trow[:, m:2 * m], in0=trow[:, 0:m],
                                         scalar1=10000.0 ** (-(m // 2) / 64.0), scalar2=None, op0=ALU.mult)
                 m = 2 * m
-            nc.vector.tensor_tensor(out=tdiag[:], in0=trow[:], in1=ident[:], op=ALU.mult)
-            nc.vector.reduce_sum(out=theta[:], in_=tdiag[:], axis=mybir.AxisListType.X)
-            nc.vector.tensor_scalar(out=turns[:], in0=theta[:], scalar1=1.0 / TWO_PI, scalar2=None, op0=ALU.mult)
-            for a in range(2):
-                cols = slice(512 * a, 512 * (a + 1))
-                nc.vector.tensor_scalar(out=kint[:, cols], in0=pos[:, cols], scalar1=turns[:, 0:1], scalar2=None,
-                                        op0=ALU.mult)
-                nc.vector.scalar_tensor_tensor(out=ang[:, cols], in0=pos[:, cols], scalar=turns[:, 0:1],
-                                               in1=kint[:, cols], op0=ALU.mult, op1=ALU.subtract)
+            nc.vector.tensor_scalar(out=turns[:], in0=trow[:], scalar1=1.0 / TWO_PI, scalar2=None, op0=ALU.mult)
             nc.vector.tensor_copy(out=sv[:, :, 0:1], in_=iv[:, :, 1:2])
             nc.vector.tensor_copy(out=sv[:, :, 1:2], in_=iv[:, :, 0:1])
             nc.vector.tensor_copy(out=bias_f[:], in_=bias_bf[:])
+            for a in range(L // P):
+                nc.vector.tensor_scalar(out=kint[:, a, :], in0=turns[:], scalar1=pos[:, a:a + 1], scalar2=None,
+                                        op0=ALU.mult)
+            for a in range(L // P):
+                nc.vector.scalar_tensor_tensor(out=ang[:, a, :], in0=turns[:], scalar=pos[:, a:a + 1],
+                                               in1=kint[:, a, :], op0=ALU.mult, op1=ALU.subtract)
 
         def tables_scalar(a):
-            cols = slice(256 * a, 256 * (a + 1))
-            nc.scalar.activation(out=aabs[:, cols], in_=ang[:, cols], func=ACT.Abs)
-            nc.scalar.activation(out=tab[:, a, 1, :], in_=ang[:, cols], func=ACT.Sin, scale=TWO_PI)
-            nc.scalar.activation(out=tab[:, a, 0, :], in_=aabs[:, cols], func=ACT.Sin, bias=math.pi / 2.0,
+            two = slice(2 * a, 2 * a + 2)
+            nc.scalar.activation(out=aabs[:, two, :], in_=ang[:, two, :], func=ACT.Abs)
+            nc.scalar.activation(out=tab_t[:, two, 1, :], in_=ang[:, two, :], func=ACT.Sin, scale=TWO_PI)
+            nc.scalar.activation(out=tab_t[:, two, 0, :], in_=aabs[:, two, :], func=ACT.Sin, bias=math.pi / 2.0,
                                  scale=-TWO_PI)
 
         wc = [const.tile([P, 4, PASSES * P], U32, name="wc%d" % a, align_bytes=64) for a in range(2)]
@@ -206,8 +202,12 @@ def tile_weightlinearattention_pa_kernel(tc, x_bytes, x_scale, w, bias, out):
 
         def fill_tables(blk):
             tabp[blk] = bank([P, 2, 256], "tabp")
-            nc.tensor.matmul(out=tabp[blk][:].rearrange("p e n -> p (e n)"), lhsT=ident[:],
-                             rhs=tab[:, blk].rearrange("p e n -> p (e n)"), start=True, stop=True)
+            for t in range(2):
+                for e in range(2):
+                    nc.tensor.transpose(tabp[blk][:, e, t * P:(t + 1) * P], tab_t[:, 2 * blk + t, e, :], ident[:])
+
+        def copy_tables(blk):
+            nc.vector.tensor_copy(out=tab[:, blk], in_=tabp[blk][:])
 
         def vec_product(dst, r, heads, blk):
             nc.vector.tensor_tensor(out=dst, in0=r.unsqueeze(1).to_broadcast([P, 2, heads, 256]),
@@ -319,11 +319,13 @@ def tile_weightlinearattention_pa_kernel(tc, x_bytes, x_scale, w, bias, out):
                 for i in range(4):
                     if k >= 1:
                         turn_out(k - 1, i // 2, False, (i % 2,))
-                    mx_relu(k + 1, (i,))
                     if i == 0 and k in (2, 4, 6):
                         fill_tables(k // 2)
+                    mx_relu(k + 1, (i,))
                     if i < 2 and 1 <= k < 6:
                         x_turn(k + 2, i, "tp")
+                if k % 2 == 0:
+                    copy_tables(k // 2)
                 product(k)
             ones = [work.tile([P, 2, 256], F32, name="one", tag="one", bufs=4) for h in range(4, 8)]
             for h in (6, 7):

@@ -33,7 +33,7 @@ def tile_weightlinearattention_pa_kernel(tc, x_bytes, x_scale, w, bias, out):
         sc_col = const.tile([P, E // P], F32, name="sc_col")
         bias_bf = const.tile([P, H], BF16, name="bias_bf")
         with nc.allow_non_contiguous_dma(reason="one value to a partition"):
-            nc.scalar.dma_start(out=sc_col[:], in_=x_scale.rearrange("a b (k p) -> p (a b k)", p=P))
+            nc.scalar.dma_start(out=sc_col[:], in_=x_scale.rearrange("a b (p k) -> p (a b k)", p=P))
             nc.scalar.dma_start(out=bias_bf[:], in_=bias.rearrange("(h d) -> d h", d=D))
 
         xb = [None] * 8
@@ -100,7 +100,8 @@ def tile_weightlinearattention_pa_kernel(tc, x_bytes, x_scale, w, bias, out):
                 for i in range(4):
                     k = 4 * b + i
                     nc.tensor.transpose(tp[:, i, :], sc_col[:, k:k + 1].to_broadcast([P, P]), ident[:])
-                nc.scalar.copy(out=scale_all[:, 512 * b:512 * (b + 1)], in_=tp[:].rearrange("p i j -> p (i j)"))
+                nc.scalar.copy(out=scale_all[:].rearrange("p (j k) -> p j k", k=E // P)[:, :, 4 * b:4 * b + 4],
+                               in_=tp[:].rearrange("p i j -> p j i"))
 
         def tables_vector():
             nc.vector.memset(trow[:, 0:1], 1.0)
@@ -111,15 +112,17 @@ def tile_weightlinearattention_pa_kernel(tc, x_bytes, x_scale, w, bias, out):
                                         scalar1=10000.0 ** (-(m // 2) / 64.0), scalar2=None, op0=ALU.mult)
                 m = 2 * m
             nc.vector.tensor_scalar(out=turns[:], in0=trow[:], scalar1=1.0 / TWO_PI, scalar2=None, op0=ALU.mult)
-            nc.vector.tensor_copy(out=sv[:, :, 0:1], in_=iv[:, :, 1:2])
-            nc.vector.tensor_copy(out=sv[:, :, 1:2], in_=iv[:, :, 0:1])
-            nc.vector.tensor_copy(out=bias_f[:], in_=bias_bf[:])
             for a in range(L // P):
                 nc.vector.tensor_scalar(out=kint[:, a, :], in0=turns[:], scalar1=pos[:, a:a + 1], scalar2=None,
                                         op0=ALU.mult)
             for a in range(L // P):
                 nc.vector.scalar_tensor_tensor(out=ang[:, a, :], in0=turns[:], scalar=pos[:, a:a + 1],
                                                in1=kint[:, a, :], op0=ALU.mult, op1=ALU.subtract)
+            nc.vector.tensor_copy(out=sv[:, :, 0:1], in_=iv[:, :, 1:2])
+            nc.vector.tensor_copy(out=sv[:, :, 1:2], in_=iv[:, :, 0:1])
+
+        def widen_bias():
+            nc.vector.tensor_copy(out=bias_f[:], in_=bias_bf[:])
 
         def tables_scalar(a):
             two = slice(2 * a, 2 * a + 2)
@@ -297,6 +300,7 @@ def tile_weightlinearattention_pa_kernel(tc, x_bytes, x_scale, w, bias, out):
                     x_turn(j, i, head_tag())
                     keep_clock(1)
             w_quant(0)
+            widen_bias()
             x_quant(0)
             for h in range(4, 8):
                 w_turn(h)
@@ -309,7 +313,7 @@ def tile_weightlinearattention_pa_kernel(tc, x_bytes, x_scale, w, bias, out):
                 x_turn(2, i, ("tp", "ot")[i])
             w_quant(1)
             mx_relu(0, (2, 3))
-            for k in range(7):
+            for k in range(6):
                 if k < 3:
                     tables_scalar(k + 1)
                 x_quant(k + 1)
@@ -319,7 +323,7 @@ def tile_weightlinearattention_pa_kernel(tc, x_bytes, x_scale, w, bias, out):
                 for i in range(4):
                     if k >= 1:
                         turn_out(k - 1, i // 2, False, (i % 2,))
-                    if i == 0 and k in (2, 4, 6):
+                    if i == 0 and k in (2, 4):
                         fill_tables(k // 2)
                     mx_relu(k + 1, (i,))
                     if i < 2 and 1 <= k < 6:
@@ -328,16 +332,29 @@ def tile_weightlinearattention_pa_kernel(tc, x_bytes, x_scale, w, bias, out):
                     copy_tables(k // 2)
                 product(k)
             ones = [work.tile([P, 2, 256], F32, name="one", tag="one", bufs=4) for h in range(4, 8)]
-            for h in (6, 7):
-                pool_product(ones[h - 4][:].unsqueeze(2), rs[15][:, h - 4:h - 3, :], 1, 3)
-            turn_out(6, 0, False)
+            x_quant(7)
+            pool_gate(6)
+            turn_out(5, 0, False, (0,))
+            fill_tables(3)
+            mx_relu(7, (0,))
+            copy_tables(3)
+            product(6)
+            turn_out(5, 0, False, (1,))
+            turn_out(5, 1, False, (0,))
+            mx_relu(7, (1,))
+            turn_out(5, 1, False, (1,))
+            turn_out(6, 0, False, (0,))
+            mx_relu(7, (2,))
             uva[7] = work.tile([P, 2, 4, 256], F32, name="uva", tag="uva", bufs=3)
             vec_product(uva[7][:], rs[14][:], 4, 3)
-            turn_out(6, 1, False)
-            last_head(7, 6, ones[2], ("y", "y"))
-            last_head(7, 7, ones[3], ("y", "tp"))
-            turn_out(7, 0, True)
-            for h in (4, 5):
+            turn_out(6, 0, False, (1,))
+            turn_out(6, 1, False, (0,))
+            mx_relu(7, (3,))
+            for h in (4, 5, 6, 7):
                 vec_product(ones[h - 4][:].unsqueeze(2), rs[15][:, h - 4:h - 3, :], 1, 3)
-                last_head(7, h, ones[h - 4], (("y", "y"), ("y", "tp"))[h - 4])
+            turn_out(6, 1, False, (1,))
+            turn_out(7, 0, False, (0,))
+            turn_out(7, 0, True, (1,))
+            for h in (4, 5, 6, 7):
+                last_head(7, h, ones[h - 4], (("y", "y"), ("y", "tp"))[h % 2])
             finish_on_vector()

@@ -287,25 +287,25 @@ def tile_weightlinearattention_pa_kernel(tc, x_bytes, x_scale, w, bias, out):
             spare.append(bank([P, 512], "tabp"))
             keep_clock(5)
             spread_scales()
-            keep_clock(1)
+            keep_clock(2)
             tables_vector()
             for h in range(4):
                 w_turn(h)
                 if h % 2 == 1:
-                    keep_clock(1)
+                    keep_clock(2)
             tables_scalar(0)
             for j in range(2):
                 x_widen(j)
                 for i in range(2):
                     x_turn(j, i, head_tag())
-                    keep_clock(1)
+                    keep_clock(2)
             w_quant(0)
             widen_bias()
             x_quant(0)
             for h in range(4, 8):
                 w_turn(h)
                 if h == 5:
-                    keep_clock(1)
+                    keep_clock(2)
             fill_tables(0)
             mx_relu(0, (0, 1))
             x_widen(2)

@@ -43,13 +43,23 @@ def tile_weightlinearattention_pa_kernel(tc, x_bytes, x_scale, w, bias, out):
             xb[q] = raw.tile([P, B, E], U8, name="xbytes%d" % q)
             nc.sync.dma_start(out=xb[q][:], in_=x_bytes[q * P:(q + 1) * P, :, :])
 
+        def load_x_half(q, c):
+            if c == 0:
+                xb[q] = raw.tile([P, B, E], U8, name="xbytes%d" % q)
+            nc.sync.dma_start(out=xb[q][:, c, :], in_=x_bytes[q * P:(q + 1) * P, c, :])
+
         def load_w(h):
             wr[h] = raw.tile([P, E], BF16, name="wraw%d" % h)
             nc.sync.dma_start(out=wr[h][:], in_=w[h * P:(h + 1) * P, :])
 
-        load_x(0)
-        load_x(1)
-        for h in range(8):
+        load_w(0)
+        load_x_half(0, 0)
+        load_x_half(1, 0)
+        for h in range(1, 5):
+            load_w(h)
+        load_x_half(0, 1)
+        load_x_half(1, 1)
+        for h in range(5, 8):
             load_w(h)
         for q in range(2, 8):
             load_x(q)
@@ -165,13 +175,15 @@ def tile_weightlinearattention_pa_kernel(tc, x_bytes, x_scale, w, bias, out):
                                   scales=ws[a][:].rearrange("p a n -> p (a n)"),
                                   in_=wg[a][:].rearrange("p a g r j -> p (a g r j)"))
 
+        def x_widen1(j, i):
+            q = 2 * (j // 2) + i
+            xw[2 * j + i] = work.tile([P, E], BF16, name="xw", tag="xw", bufs=4)
+            nc.vector.tensor_tensor(out=xw[2 * j + i][:], in0=xb[q][:, j % 2, :].bitcast(FP8),
+                                    in1=scale_all[:], op=ALU.mult)
+
         def x_widen(j):
-            c = j % 2
             for i in range(2):
-                q = 2 * (j // 2) + i
-                xw[2 * j + i] = work.tile([P, E], BF16, name="xw", tag="xw", bufs=4)
-                nc.vector.tensor_tensor(out=xw[2 * j + i][:], in0=xb[q][:, c, :].bitcast(FP8),
-                                        in1=scale_all[:], op=ALU.mult)
+                x_widen1(j, i)
 
         def x_turn(j, i, tag):
             if i == 0:
@@ -221,7 +233,7 @@ def tile_weightlinearattention_pa_kernel(tc, x_bytes, x_scale, w, bias, out):
                                     in1=tab[:, blk].unsqueeze(2).to_broadcast([P, 2, heads, 256]), op=ALU.mult)
 
         def pool_gate(k):
-            if 1 <= k < 6:
+            if k < 6:
                 nc.gpsimd.tensor_copy(out=junk_bf[:], in_=xw[2 * (k + 2) + 1][:, 0:16])
             else:
                 nc.gpsimd.tensor_copy(out=junk[:], in_=xc[k + 1][:, 0, 0:16])
@@ -287,38 +299,39 @@ def tile_weightlinearattention_pa_kernel(tc, x_bytes, x_scale, w, bias, out):
             spare.append(bank([P, 512], "tabp"))
             keep_clock(5)
             spread_scales()
-            keep_clock(2)
             tables_vector()
-            for h in range(4):
-                w_turn(h)
-                if h % 2 == 1:
-                    keep_clock(2)
-            tables_scalar(0)
-            for j in range(2):
-                x_widen(j)
-                for i in range(2):
-                    x_turn(j, i, head_tag())
-                    keep_clock(2)
+            w_turn(0)
+            keep_clock(2)
+            w_turn(1)
+            w_turn(2)
+            w_turn(3)
+            keep_clock(2)
+            x_widen1(0, 0)
+            x_turn(0, 0, head_tag())
+            w_turn(4)
+            x_widen1(0, 1)
+            x_turn(0, 1, head_tag())
+            keep_clock(2)
             w_quant(0)
+            w_turn(5)
+            w_turn(6)
+            w_turn(7)
+            x_widen1(1, 0)
             widen_bias()
             x_quant(0)
-            for h in range(4, 8):
-                w_turn(h)
-                if h == 5:
-                    keep_clock(2)
-            fill_tables(0)
+            x_turn(1, 0, "tp")
             mx_relu(0, (0, 1))
-            x_widen(2)
-            for i in range(2):
-                x_turn(2, i, ("tp", "ot")[i])
+            x_widen1(1, 1)
+            x_turn(1, 1, "ot")
+            tables_scalar(0)
             w_quant(1)
             mx_relu(0, (2, 3))
+            fill_tables(0)
             for k in range(6):
                 if k < 3:
                     tables_scalar(k + 1)
                 x_quant(k + 1)
-                if 1 <= k < 6:
-                    x_widen(k + 2)
+                x_widen(k + 2)
                 pool_gate(k)
                 for i in range(4):
                     if k >= 1:
@@ -326,7 +339,7 @@ def tile_weightlinearattention_pa_kernel(tc, x_bytes, x_scale, w, bias, out):
                     if i == 0 and k in (2, 4):
                         fill_tables(k // 2)
                     mx_relu(k + 1, (i,))
-                    if i < 2 and 1 <= k < 6:
+                    if i < 2:
                         x_turn(k + 2, i, "tp")
                 if k % 2 == 0:
                     copy_tables(k // 2)

@@ -299,23 +299,26 @@ def tile_weightlinearattention_pa_kernel(tc, x_bytes, x_scale, w, bias, out):
             spare.append(bank([P, 512], "tabp"))
             keep_clock(5)
             spread_scales()
+            keep_clock(2)
             tables_vector()
             w_turn(0)
-            keep_clock(2)
             w_turn(1)
+            keep_clock(2)
             w_turn(2)
             w_turn(3)
             keep_clock(2)
             x_widen1(0, 0)
             x_turn(0, 0, head_tag())
             w_turn(4)
+            keep_clock(2)
             x_widen1(0, 1)
             x_turn(0, 1, head_tag())
+            w_turn(5)
             keep_clock(2)
             w_quant(0)
-            w_turn(5)
             w_turn(6)
             w_turn(7)
+            keep_clock(2)
             x_widen1(1, 0)
             widen_bias()
             x_quant(0)
@@ -333,13 +336,14 @@ def tile_weightlinearattention_pa_kernel(tc, x_bytes, x_scale, w, bias, out):
                 x_quant(k + 1)
                 x_widen(k + 2)
                 pool_gate(k)
-                for i in range(4):
-                    if k >= 1:
+                for what, i in (("O", 0), ("O", 1), ("M", 0), ("M", 1), ("X", 0), ("O", 2), ("M", 2), ("X", 1), ("O", 3), ("M", 3)):
+                    if what == "O" and k >= 1:
                         turn_out(k - 1, i // 2, False, (i % 2,))
-                    if i == 0 and k in (2, 4):
+                    if what == "O" and i == 0 and k in (2, 4):
                         fill_tables(k // 2)
-                    mx_relu(k + 1, (i,))
-                    if i < 2:
+                    if what == "M":
+                        mx_relu(k + 1, (i,))
+                    if what == "X":
                         x_turn(k + 2, i, "tp")
                 if k % 2 == 0:
                     copy_tables(k // 2)

@@ -134,12 +134,19 @@ def tile_weightlinearattention_pa_kernel(tc, x_bytes, x_scale, w, bias, out):
         def widen_bias():
             nc.vector.tensor_copy(out=bias_f[:], in_=bias_bf[:])
 
-        def tables_scalar(a):
+        def tables_part(a, part):
             two = slice(2 * a, 2 * a + 2)
-            nc.scalar.activation(out=aabs[:, two, :], in_=ang[:, two, :], func=ACT.Abs)
-            nc.scalar.activation(out=tab_t[:, two, 1, :], in_=ang[:, two, :], func=ACT.Sin, scale=TWO_PI)
-            nc.scalar.activation(out=tab_t[:, two, 0, :], in_=aabs[:, two, :], func=ACT.Sin, bias=math.pi / 2.0,
-                                 scale=-TWO_PI)
+            if part == 0:
+                nc.scalar.activation(out=aabs[:, two, :], in_=ang[:, two, :], func=ACT.Abs)
+            if part == 1:
+                nc.scalar.activation(out=tab_t[:, two, 1, :], in_=ang[:, two, :], func=ACT.Sin, scale=TWO_PI)
+            if part == 2:
+                nc.scalar.activation(out=tab_t[:, two, 0, :], in_=aabs[:, two, :], func=ACT.Sin, bias=math.pi / 2.0,
+                                     scale=-TWO_PI)
+
+        def tables_scalar(a):
+            for part in range(3):
+                tables_part(a, part)
 
         wc = [const.tile([P, 4, PASSES * P], U32, name="wc%d" % a, align_bytes=64) for a in range(2)]
         ws = [const.tile([P, 4, PASSES * P], U8, name="ws%d" % a, align_bytes=64) for a in range(2)]
@@ -233,7 +240,7 @@ def tile_weightlinearattention_pa_kernel(tc, x_bytes, x_scale, w, bias, out):
                                     in1=tab[:, blk].unsqueeze(2).to_broadcast([P, 2, heads, 256]), op=ALU.mult)
 
         def pool_gate(k):
-            if k < 6:
+            if 1 <= k < 6:
                 nc.gpsimd.tensor_copy(out=junk_bf[:], in_=xw[2 * (k + 2) + 1][:, 0:16])
             else:
                 nc.gpsimd.tensor_copy(out=junk[:], in_=xc[k + 1][:, 0, 0:16])
@@ -304,37 +311,44 @@ def tile_weightlinearattention_pa_kernel(tc, x_bytes, x_scale, w, bias, out):
             w_turn(0)
             w_turn(1)
             keep_clock(2)
+            tables_part(0, 0)
             w_turn(2)
             w_turn(3)
             keep_clock(2)
+            tables_part(0, 1)
             x_widen1(0, 0)
             x_turn(0, 0, head_tag())
             w_turn(4)
             keep_clock(2)
+            tables_part(0, 2)
             x_widen1(0, 1)
             x_turn(0, 1, head_tag())
             w_turn(5)
             keep_clock(2)
+            x_widen1(1, 0)
             w_quant(0)
             w_turn(6)
             w_turn(7)
             keep_clock(2)
-            x_widen1(1, 0)
+            x_widen1(1, 1)
             widen_bias()
             x_quant(0)
             x_turn(1, 0, "tp")
-            mx_relu(0, (0, 1))
-            x_widen1(1, 1)
             x_turn(1, 1, "ot")
-            tables_scalar(0)
-            w_quant(1)
-            mx_relu(0, (2, 3))
             fill_tables(0)
+            mx_relu(0, (0, 1))
+            x_widen1(2, 0)
+            w_quant(1)
+            x_turn(2, 0, "tp")
+            mx_relu(0, (2, 3))
+            x_widen1(2, 1)
+            x_turn(2, 1, "ot")
             for k in range(6):
                 if k < 3:
                     tables_scalar(k + 1)
                 x_quant(k + 1)
-                x_widen(k + 2)
+                if 1 <= k < 6:
+                    x_widen(k + 2)
                 pool_gate(k)
                 for what, i in (("O", 0), ("O", 1), ("M", 0), ("M", 1), ("X", 0), ("O", 2), ("M", 2), ("X", 1), ("O", 3), ("M", 3)):
                     if what == "O" and k >= 1:
@@ -343,7 +357,7 @@ def tile_weightlinearattention_pa_kernel(tc, x_bytes, x_scale, w, bias, out):
                         fill_tables(k // 2)
                     if what == "M":
                         mx_relu(k + 1, (i,))
-                    if what == "X":
+                    if what == "X" and 1 <= k < 6:
                         x_turn(k + 2, i, "tp")
                 if k % 2 == 0:
                     copy_tables(k // 2)

@@ -329,23 +329,20 @@ def tile_weightlinearattention_pa_kernel(tc, x_bytes, x_scale, w, bias, out):
             w_quant(0)
             w_turn(6)
             w_turn(7)
-            keep_clock(2)
             x_widen1(1, 1)
             widen_bias()
             x_quant(0)
+            mx_relu(0, (0, 1))
             x_turn(1, 0, "tp")
             x_turn(1, 1, "ot")
             fill_tables(0)
-            mx_relu(0, (0, 1))
             x_widen1(2, 0)
             w_quant(1)
-            x_turn(2, 0, "tp")
             mx_relu(0, (2, 3))
             x_widen1(2, 1)
+            x_turn(2, 0, "tp")
             x_turn(2, 1, "ot")
             for k in range(6):
-                if k < 3:
-                    tables_scalar(k + 1)
                 x_quant(k + 1)
                 if 1 <= k < 6:
                     x_widen(k + 2)
@@ -359,6 +356,8 @@ def tile_weightlinearattention_pa_kernel(tc, x_bytes, x_scale, w, bias, out):
                         mx_relu(k + 1, (i,))
                     if what == "X" and 1 <= k < 6:
                         x_turn(k + 2, i, "tp")
+                if k < 3:
+                    tables_scalar(k + 1)
                 if k % 2 == 0:
                     copy_tables(k // 2)
                 product(k)

@@ -304,7 +304,7 @@ def tile_weightlinearattention_pa_kernel(tc, x_bytes, x_scale, w, bias, out):
             nc.scalar.activation(out=warm[:], in_=zero[:], func=ACT.Sin)
             nc.vector.memset(idle[:], 0.0)
             spare.append(bank([P, 512], "tabp"))
-            keep_clock(5)
+            keep_clock(4)
             spread_scales()
             keep_clock(2)
             tables_vector()

from contextlib import ExitStack
import math

import concourse.mybir as mybir
from concourse.masks import make_identity

L, B, E, H, D = 1024, 2, 1024, 8, 128
FLOPS = 2 * L * B * E * H * D

F32 = mybir.dt.float32
BF16 = mybir.dt.bfloat16
U8 = mybir.dt.uint8
U32 = mybir.dt.uint32
I32 = mybir.dt.int32
FP8 = mybir.dt.float8_e4m3fn
FP8X4 = mybir.dt.float8_e4m3fn_x4
ALU = mybir.AluOpType
ACT = mybir.ActivationFunctionType

P = 128
PASSES = E // 512
TWO_PI = 2.0 * math.pi


def tile_weightlinearattention_pa_kernel(tc, x_bytes, x_scale, w, bias, out):
    nc = tc.nc
    with ExitStack() as ctx:
        const = ctx.enter_context(tc.tile_pool(name="const", bufs=1))
        raw = ctx.enter_context(tc.tile_pool(name="raw", bufs=1))
        work = ctx.enter_context(tc.tile_pool(name="work", bufs=2))
        psum = ctx.enter_context(tc.psum_pool(name="psum", bufs=2))

        sc_col = const.tile([P, E // P], F32, name="sc_col")
        bias_bf = const.tile([P, H], BF16, name="bias_bf")
        with nc.allow_non_contiguous_dma(reason="one value to a partition"):
            nc.scalar.dma_start(out=sc_col[:], in_=x_scale.rearrange("a b (p k) -> p (a b k)", p=P))
            nc.scalar.dma_start(out=bias_bf[:], in_=bias.rearrange("(h d) -> d h", d=D))

        xb = [None] * 8
        wr = [None] * 8

        def load_x(q):
            xb[q] = raw.tile([P, B, E], U8, name="xbytes%d" % q)
            nc.sync.dma_start(out=xb[q][:], in_=x_bytes[q * P:(q + 1) * P, :, :])

        def load_x_half(q, c):
            if c == 0:
                xb[q] = raw.tile([P, B, E], U8, name="xbytes%d" % q)
            nc.sync.dma_start(out=xb[q][:, c, :], in_=x_bytes[q * P:(q + 1) * P, c, :])

        def load_w(h):
            wr[h] = raw.tile([P, E], BF16, name="wraw%d" % h)
            nc.sync.dma_start(out=wr[h][:], in_=w[h * P:(h + 1) * P, :])

        load_w(0)
        load_x_half(0, 0)
        load_x_half(1, 0)
        for h in range(1, 5):
            load_w(h)
        load_x_half(0, 1)
        load_x_half(1, 1)
        for h in range(5, 8):
            load_w(h)
        for q in range(2, 8):
            load_x(q)

        zero = const.tile([P, 1], F32, name="zero")
        nc.gpsimd.memset(zero[:], 0.0)
        ident = const.tile([P, P], F32, name="ident")
        make_identity(nc, ident[:])
        swap = const.tile([P, P], F32, name="swap")
        iv = ident[:].rearrange("p (i e) -> p i e", e=2)
        sv = swap[:].rearrange("p (i e) -> p i e", e=2)
        pos = const.tile([P, L // P], F32, name="pos")
        nc.gpsimd.iota(pos[:], pattern=[[P, L // P]], base=0, channel_multiplier=1,
                       allow_small_or_imprecise_dtypes=True)

        scale_all = const.tile([P, E], F32, name="scale_all")
        warm = const.tile([P, 1], F32, name="warm")
        trow = const.tile([P, D], F32, name="trow")
        turns = const.tile([P, D], F32, name="turns")
        kint = const.tile([P, L // P, D], I32, name="kint")
        ang = const.tile([P, L // P, D], F32, name="ang")
        aabs = const.tile([P, L // P, D], F32, name="aabs")
        tab_t = const.tile([P, L // P, 2, D], F32, name="tab_t")
        tab = const.tile([P, 4, 2, 256], F32, name="tab")
        idle = const.tile([P, 512], BF16, name="idle")
        junk = const.tile([P, 16], U32, name="junk")
        junk_bf = const.tile([P, 16], BF16, name="junk_bf")
        bias_f = const.tile([P, H], F32, name="bias_f")

        depth = {"tabp": 1, "tp": 1, "y": 3, "ot": 3}
        head_cycle = ["tp", "ot", "y", "ot", "y", "ot", "y"]
        head_used = []

        def head_tag():
            head_used.append(0)
            return head_cycle[(len(head_used) - 1) % len(head_cycle)]

        def bank(shape, tag):
            return psum.tile(shape, F32, name=tag, tag=tag, bufs=depth[tag])

        def keep_clock(n):
            for i in range(n):
                nc.tensor.matmul(out=spare[0][:], lhsT=idle[:, 0:P], rhs=idle[:], start=True, stop=True)

        def spread_scales():
            for b in range(2):
                tp = bank([P, 4, P], head_tag())
                for i in range(4):
                    k = 4 * b + i
                    nc.tensor.transpose(tp[:, i, :], sc_col[:, k:k + 1].to_broadcast([P, P]), ident[:])
                nc.scalar.copy(out=scale_all[:].rearrange("p (j k) -> p j k", k=E // P)[:, :, 4 * b:4 * b + 4],
                               in_=tp[:].rearrange("p i j -> p j i"))

        def tables_vector():
            nc.vector.memset(trow[:, 0:1], 1.0)
            nc.vector.memset(trow[:, 1:2], -1.0)
            m = 2
            while m < D:
                nc.vector.tensor_scalar(out=trow[:, m:2 * m], in0=trow[:, 0:m],
                                        scalar1=10000.0 ** (-(m // 2) / 64.0), scalar2=None, op0=ALU.mult)
                m = 2 * m
            nc.vector.tensor_scalar(out=turns[:], in0=trow[:], scalar1=1.0 / TWO_PI, scalar2=None, op0=ALU.mult)
            for a in range(L // P):
                nc.vector.tensor_scalar(out=kint[:, a, :], in0=turns[:], scalar1=pos[:, a:a + 1], scalar2=None,
                                        op0=ALU.mult)
            for a in range(L // P):
                nc.vector.scalar_tensor_tensor(out=ang[:, a, :], in0=turns[:], scalar=pos[:, a:a + 1],
                                               in1=kint[:, a, :], op0=ALU.mult, op1=ALU.subtract)
            nc.vector.tensor_copy(out=sv[:, :, 0:1], in_=iv[:, :, 1:2])
            nc.vector.tensor_copy(out=sv[:, :, 1:2], in_=iv[:, :, 0:1])

        def widen_bias():
            nc.vector.tensor_copy(out=bias_f[:], in_=bias_bf[:])

        def tables_part(a, part):
            two = slice(2 * a, 2 * a + 2)
            if part == 0:
                nc.scalar.activation(out=aabs[:, two, :], in_=ang[:, two, :], func=ACT.Abs)
            if part == 1:
                nc.scalar.activation(out=tab_t[:, two, 1, :], in_=ang[:, two, :], func=ACT.Sin, scale=TWO_PI)
            if part == 2:
                nc.scalar.activation(out=tab_t[:, two, 0, :], in_=aabs[:, two, :], func=ACT.Sin, bias=math.pi / 2.0,
                                     scale=-TWO_PI)

        def tables_scalar(a):
            for part in range(3):
                tables_part(a, part)

        wc = [const.tile([P, 4, PASSES * P], U32, name="wc%d" % a, align_bytes=64) for a in range(2)]
        ws = [const.tile([P, 4, PASSES * P], U8, name="ws%d" % a, align_bytes=64) for a in range(2)]
        xc = [const.tile([P, PASSES, 256], U32, name="xc%d" % j, align_bytes=64) for j in range(8)]
        xs = [const.tile([P, PASSES, 256], U8, name="xs%d" % j, align_bytes=64) for j in range(8)]
        wg = [None] * 8
        xw = [None] * 16
        xg = [None] * 8
        rs = [None] * 32
        uva = [None] * 8
        uvb = [None] * 8
        uvg = [None] * 8
        tabp = [None] * 4
        spare = []
        later = []

        def turn(src, tag):
            words = src.bitcast(F32)
            tp = bank([P, PASSES, 2, P], tag)
            for g in range(PASSES):
                for u in range(2):
                    nc.tensor.transpose(tp[:, g, u, :], words[:, 256 * g + u:256 * (g + 1):2], ident[:])
            return tp

        def w_turn(h):
            tp = turn(wr[h][:], head_tag())
            if h % 4 == 0:
                wg[h // 4] = work.tile([P, 4, PASSES, P, 4], BF16, name="wg", tag="wg", bufs=2, align_bytes=64)
            nc.scalar.copy(out=wg[h // 4][:, h % 4].bitcast(F32), in_=tp[:].rearrange("p g u r -> p g r u"))

        def w_quant(a):
            nc.vector.quantize_mx(out=wc[a][:].rearrange("p a n -> p (a n)").bitcast(FP8X4),
                                  scales=ws[a][:].rearrange("p a n -> p (a n)"),
                                  in_=wg[a][:].rearrange("p a g r j -> p (a g r j)"))

        def x_widen1(j, i):
            q = 2 * (j // 2) + i
            xw[2 * j + i] = work.tile([P, E], BF16, name="xw", tag="xw", bufs=4)
            nc.vector.tensor_tensor(out=xw[2 * j + i][:], in0=xb[q][:, j % 2, :].bitcast(FP8),
                                    in1=scale_all[:], op=ALU.mult)

        def x_widen(j):
            for i in range(2):
                x_widen1(j, i)

        def x_turn(j, i, tag):
            if i == 0:
                xg[j] = work.tile([P, PASSES, 2, P, 4], BF16, name="xg", tag="xg", bufs=3, align_bytes=64)
            tp = turn(xw[2 * j + i][:], tag)
            nc.scalar.copy(out=xg[j][:, :, i, :, :].bitcast(F32), in_=tp[:].rearrange("p g u r -> p g r u"))

        def x_quant(j):
            nc.vector.quantize_mx(out=xc[j][:].rearrange("p g n -> p (g n)").bitcast(FP8X4),
                                  scales=xs[j][:].rearrange("p g n -> p (g n)"),
                                  in_=xg[j][:].rearrange("p g t r j -> p (g t r j)"))

        def mx_relu(j, pairs):
            for hp in pairs:
                y = bank([P, 2, 256], "y")
                for hh in range(2):
                    h = 2 * hp + hh
                    for g in range(PASSES):
                        nc.tensor.matmul_mx(out=y[:, hh, :],
                                            lhsT=wc[h // 4][:, h % 4, g * P:(g + 1) * P].bitcast(FP8X4),
                                            lhsT_scale=ws[h // 4][:, h % 4, g * P:(g + 1) * P],
                                            rhs=xc[j][:, g, :].bitcast(FP8X4),
                                            rhs_scale=xs[j][:, g, :],
                                            start=(g == 0), stop=(g == PASSES - 1))
                if hp % 2 == 0:
                    rs[2 * j + hp // 2] = work.tile([P, 4, 256], F32, name="r", tag="r", bufs=6)
                for hh in range(2):
                    h = 2 * hp + hh
                    nc.scalar.activation(out=rs[2 * j + hp // 2][:, h % 4, :], in_=y[:, hh, :], func=ACT.Relu,
                                         bias=bias_f[:, h:h + 1], scale=1.0)

        def fill_tables(blk):
            tabp[blk] = bank([P, 2, 256], "tabp")
            for t in range(2):
                for e in range(2):
                    nc.tensor.transpose(tabp[blk][:, e, t * P:(t + 1) * P], tab_t[:, 2 * blk + t, e, :], ident[:])

        def copy_tables(blk):
            nc.vector.tensor_copy(out=tab[:, blk], in_=tabp[blk][:])

        def vec_product(dst, r, heads, blk):
            nc.vector.tensor_tensor(out=dst, in0=r.unsqueeze(1).to_broadcast([P, 2, heads, 256]),
                                    in1=tabp[blk][:].unsqueeze(2).to_broadcast([P, 2, heads, 256]), op=ALU.mult)

        def pool_product(dst, r, heads, blk):
            nc.gpsimd.tensor_tensor(out=dst, in0=r.unsqueeze(1).to_broadcast([P, 2, heads, 256]),
                                    in1=tab[:, blk].unsqueeze(2).to_broadcast([P, 2, heads, 256]), op=ALU.mult)

        def pool_gate(k):
            if 1 <= k < 6:
                nc.gpsimd.tensor_copy(out=junk_bf[:], in_=xw[2 * (k + 2) + 1][:, 0:16])
            else:
                nc.gpsimd.tensor_copy(out=junk[:], in_=xc[k + 1][:, 0, 0:16])

        def product(j):
            blk = j // 2
            uva[j] = work.tile([P, 2, 4, 256], F32, name="uva", tag="uva", bufs=3)
            uvb[j] = work.tile([P, 2, 2, 256], F32, name="uvb", tag="uvb", bufs=3)
            uvg[j] = work.tile([P, 2, 2, 256], F32, name="uvg", tag="uvg", bufs=3)
            pool_product(uvg[j][:], rs[2 * j + 1][:, 2:4, :], 2, blk)
            vec_product(uva[j][:], rs[2 * j][:], 4, blk)
            vec_product(uvb[j][:], rs[2 * j + 1][:, 0:2, :], 2, blk)

        def head_src(j, h):
            if h < 4:
                return uva[j][:, :, h, :]
            if h < 6:
                return uvb[j][:, :, h - 4, :]
            return uvg[j][:, :, h - 6, :]

        def add_turned(dst, both, t):
            nc.tensor.matmul(out=dst, lhsT=both[:, 0, t * P:(t + 1) * P], rhs=ident[:],
                             is_transpose=True, start=True, stop=False)
            nc.tensor.matmul(out=dst, lhsT=both[:, 1, t * P:(t + 1) * P], rhs=swap[:],
                             is_transpose=True, start=False, stop=True)

        def last_head(j, h, both, tags):
            c = j % 2
            n0 = 256 * (j // 2)
            for t in range(2):
                ot = bank([P, P], tags[t])
                add_turned(ot[:], both, t)
                o = work.tile([P, P], F32, name="os", tag="os", bufs=8)
                nc.scalar.copy(out=o[:], in_=ot[:])
                nt = n0 + t * P
                nc.sync.dma_start(out=out[c, h, nt:nt + P, :], in_=o[:])

        def turn_out(j, quad, on_vector, tiles=(0, 1)):
            c = j % 2
            for t in tiles:
                ot = bank([P, 4, P], "ot")
                for k in range(4):
                    add_turned(ot[:, k, :], head_src(j, 4 * quad + k), t)
                nt = 256 * (j // 2) + t * P
                dst = out[c, 4 * quad:4 * quad + 4, nt:nt + P, :].rearrange("h n d -> n h d")
                if on_vector:
                    later.append((ot, dst))
                else:
                    o = work.tile([P, 4, P], F32, name="o", tag="o", bufs=8)
                    nc.scalar.copy(out=o[:], in_=ot[:])
                    nc.sync.dma_start(out=dst, in_=o[:])

        def finish_on_vector():
            for ot, dst in later:
                o = work.tile([P, 4, P], F32, name="o", tag="o", bufs=8)
                nc.vector.tensor_copy(out=o[:], in_=ot[:])
                nc.sync.dma_start(out=dst, in_=o[:])
            later.clear()

        with tc.manual_schedule():
            nc.scalar.activation(out=warm[:], in_=zero[:], func=ACT.Sin)
            nc.vector.memset(idle[:], 0.0)
            spare.append(bank([P, 512], "tabp"))
            keep_clock(4)
            spread_scales()
            keep_clock(2)
            tables_vector()
            w_turn(0)
            w_turn(1)
            keep_clock(2)
            tables_part(0, 0)
            w_turn(2)
            w_turn(3)
            keep_clock(2)
            tables_part(0, 1)
            x_widen1(0, 0)
            x_turn(0, 0, head_tag())
            w_turn(4)
            keep_clock(2)
            tables_part(0, 2)
            x_widen1(0, 1)
            x_turn(0, 1, head_tag())
            w_turn(5)
            keep_clock(2)
            x_widen1(1, 0)
            w_quant(0)
            w_turn(6)
            w_turn(7)
            x_widen1(1, 1)
            widen_bias()
            x_quant(0)
            mx_relu(0, (0, 1))
            x_turn(1, 0, "tp")
            x_turn(1, 1, "ot")
            fill_tables(0)
            x_widen1(2, 0)
            w_quant(1)
            mx_relu(0, (2, 3))
            x_widen1(2, 1)
            x_turn(2, 0, "tp")
            x_turn(2, 1, "ot")
            for k in range(6):
                x_quant(k + 1)
                if 1 <= k < 6:
                    x_widen(k + 2)
                pool_gate(k)
                for what, i in (("O", 0), ("O", 1), ("M", 0), ("M", 1), ("X", 0), ("O", 2), ("M", 2), ("X", 1), ("O", 3), ("M", 3)):
                    if what == "O" and k >= 1:
                        turn_out(k - 1, i // 2, False, (i % 2,))
                    if what == "O" and i == 0 and k in (2, 4):
                        fill_tables(k // 2)
                    if what == "M":
                        mx_relu(k + 1, (i,))
                    if what == "X" and 1 <= k < 6:
                        x_turn(k + 2, i, "tp")
                if k < 3:
                    tables_scalar(k + 1)
                if k % 2 == 0:
                    copy_tables(k // 2)
                product(k)
            ones = [work.tile([P, 2, 256], F32, name="one", tag="one", bufs=4) for h in range(4, 8)]
            x_quant(7)
            pool_gate(6)
            turn_out(5, 0, False, (0,))
            fill_tables(3)
            mx_relu(7, (0,))
            copy_tables(3)
            product(6)
            turn_out(5, 0, False, (1,))
            turn_out(5, 1, False, (0,))
            mx_relu(7, (1,))
            turn_out(5, 1, False, (1,))
            turn_out(6, 0, False, (0,))
            mx_relu(7, (2,))
            uva[7] = work.tile([P, 2, 4, 256], F32, name="uva", tag="uva", bufs=3)
            vec_product(uva[7][:], rs[14][:], 4, 3)
            turn_out(6, 0, False, (1,))
            turn_out(6, 1, False, (0,))
            mx_relu(7, (3,))
            for h in (4, 5, 6, 7):
                vec_product(ones[h - 4][:].unsqueeze(2), rs[15][:, h - 4:h - 3, :], 1, 3)
            turn_out(6, 1, False, (1,))
            turn_out(7, 0, False, (0,))
            turn_out(7, 0, True, (1,))
            for h in (4, 5, 6, 7):
                last_head(7, h, ones[h - 4], (("y", "y"), ("y", "tp"))[h % 2])
            finish_on_vector()
